import numpy as np
import ml_dtypes


def mxq(x, axis, fmt="e4m3"):
    dtype, down = {"e4m3": (ml_dtypes.float8_e4m3fn, 7), "e5m2": (ml_dtypes.float8_e5m2, 14)}[fmt]
    v = np.moveaxis(np.asarray(x, np.float32).astype(ml_dtypes.bfloat16).astype(np.float64), axis, -1)
    blocks = v.reshape(v.shape[:-1] + (-1, 32))
    amax = np.abs(blocks).max(-1, keepdims=True)
    byte = np.maximum(np.where(amax > 0, np.frexp(amax)[1] - 1 + 127, 0) - down, 1)
    scale = np.exp2(byte - 127.0)
    codes = (blocks / scale).astype(np.float32).astype(dtype).astype(np.float64)
    return np.moveaxis((codes * scale).reshape(v.shape), -1, axis)


WIDE = False


def mx_kscale(k):
    if not WIDE:
        return np.ones(k)
    levels = np.array([10, -10, 5, -5, 0])
    a = np.random.permutation(np.resize(levels, k // 512 * 4)).reshape(k // 512, 4)
    idx = np.arange(k)
    return np.exp2(a[idx // 512, idx % 128 // 32])


BF16 = ml_dtypes.bfloat16


def bf(x):
    return np.asarray(x, np.float32).astype(BF16)


def f64(x):
    return np.asarray(x).astype(np.float64)


B, N, D, C, H, NS = 2, 512, 512, 256, 16, 10
HD = C // H
D4 = (0.4829629131445341, 0.8365163037378079, 0.2241438680420134, -0.1294095225512604)


def causal_multiscale(x_c, scale_gain):
    g = np.exp(scale_gain - scale_gain.max(0, keepdims=True))
    gains = g / g.sum(0, keepdims=True)
    gains_exp = np.repeat(gains, HD, axis=1)
    out = np.zeros_like(x_c)
    for j in range(NS):
        d = 2 ** j
        xp = np.pad(x_c, ((0, 0), (0, 0), (3 * d, 0)))
        y = (D4[0] * xp[:, :, 0 * d:0 * d + N]
             + D4[1] * xp[:, :, 1 * d:1 * d + N]
             + D4[2] * xp[:, :, 2 * d:2 * d + N]
             + D4[3] * xp[:, :, 3 * d:3 * d + N])
        out = out + gains_exp[j][None, :, None] * y
    return out


def setup_inputs():
    s = mx_kscale(D)
    return {"x": bf(np.random.standard_normal((B, N, D)) * s),
            "k_w": bf(np.random.standard_normal((C, D)) / np.sqrt(D) / s[None, :]),
            "k_b": bf(np.random.standard_normal(C) * 0.2),
            "v_w": bf(np.random.standard_normal((C, D)) / np.sqrt(D) / s[None, :]),
            "v_b": bf(np.random.standard_normal(C) * 0.2),
            "scale_gain": bf(np.random.standard_normal((NS, H)) * 0.5)}


def reference(x, k_w, k_b, v_w, v_b, scale_gain):
    xq = mxq(f64(x), 2, "e4m3")
    k = ((xq @ mxq(f64(k_w), 1, "e4m3").T) + f64(k_b)).reshape(B, N, H, HD)
    v = ((xq @ mxq(f64(v_w), 1, "e4m3").T) + f64(v_b)).reshape(B, N, H, HD)
    k_mag = np.sqrt((k * k).sum(-1, keepdims=True))
    field = v * k_mag
    x_c = field.transpose(0, 2, 3, 1).reshape(B, C, N)
    return causal_multiscale(x_c, f64(scale_gain))

@@ -1,0 +1,279 @@
+from contextlib import ExitStack
+
+import concourse.mybir as mybir
+from concourse.masks import make_identity
+
+F32 = mybir.dt.float32
+BF16 = mybir.dt.bfloat16
+U32 = mybir.dt.uint32
+U8 = mybir.dt.uint8
+FP8X4 = mybir.dt.float8_e4m3fn_x4
+ALU = mybir.AluOpType
+ACT = mybir.ActivationFunctionType
+AXIS = mybir.AxisListType
+
+P = 128
+BATCH, TOKENS, WIDTH, CHANNELS, HEADS, SCALES = 2, 512, 512, 256, 16, 10
+HEAD_DIM = CHANNELS // HEADS
+HALVES = CHANNELS // P
+HEADS_PER_HALF = P // HEAD_DIM
+TOKEN_BLOCKS = TOKENS // P
+TAPS = (0.4829629131445341, 0.8365163037378079, 0.2241438680420134, -0.1294095225512604)
+
+FLOPS = 2 * BATCH * TOKENS * WIDTH * 2 * CHANNELS
+
+POW2_SHIFTS = [2**i for i in range(SCALES) if 2**i < TOKENS]
+TRIPLE_SHIFTS = [3 * 2**j for j in range(SCALES) if 3 * 2**j < TOKENS]
+TERMS = sorted(
+    [(s, i) for i, s in enumerate(POW2_SHIFTS)]
+    + [(s, len(POW2_SHIFTS) + j) for j, s in enumerate(TRIPLE_SHIFTS)]
+)
+POOL_MIN_SHIFT = 48
+VECTOR_TERMS = [term for term in TERMS if term[0] < POOL_MIN_SHIFT]
+POOL_TERMS = [term for term in TERMS if term[0] >= POOL_MIN_SHIFT]
+
+
+def turn_pair(nc, pools, rows_bf16, pair, ident_f32, grouped):
+    words = rows_bf16.bitcast(F32)
+    turned = pools["work"].tile([P, 2, 2 * P], F32, name="turned", tag="work")
+    for u in range(2):
+        for a in range(2):
+            nc.tensor.transpose(
+                turned[:, u, a * P : (a + 1) * P],
+                words[:, 2 * pair + a, u * P : (u + 1) * P],
+                ident_f32,
+            )
+    nc.vector.tensor_copy(
+        out=grouped.bitcast(F32)[:, 2 * pair * P : 2 * (pair + 1) * P, :],
+        in_=turned[:].rearrange("p u c -> p c u"),
+    )
+
+
+def quantise(nc, grouped, codes, scales):
+    nc.vector.quantize_mx(
+        out=codes.bitcast(FP8X4), scales=scales, in_=grouped.rearrange("p c t -> p (c t)")
+    )
+
+
+def tile_causalwaveletfieldattentionbyte_pa_s_kernel(
+    tc, x, k_w, k_b, v_w, v_b, scale_gain, out
+):
+    nc = tc.nc
+    with ExitStack() as stack:
+        pools = {
+            "const": stack.enter_context(tc.tile_pool(name="const", bufs=1)),
+            "unit": stack.enter_context(tc.tile_pool(name="unit", bufs=BATCH * HALVES)),
+            "plane": stack.enter_context(tc.tile_pool(name="plane", bufs=4)),
+            "work": stack.enter_context(tc.psum_pool(name="work", bufs=4)),
+            "field": stack.enter_context(tc.psum_pool(name="field", bufs=1)),
+        }
+        const = pools["const"]
+
+        vec_rows = const.tile([P, P], BF16, name="vec_rows")
+        nc.vector.memset(vec_rows[:], 0.0)
+        nc.scalar.dma_start(out=vec_rows[0:2, :], in_=k_b.rearrange("(a c) -> a c", c=P))
+        nc.scalar.dma_start(out=vec_rows[2:4, :], in_=v_b.rearrange("(a c) -> a c", c=P))
+        with nc.allow_non_contiguous_dma(reason="160 gains, one to each head's first channel"):
+            for h in range(HALVES):
+                nc.scalar.dma_start(
+                    out=vec_rows[4 + SCALES * h : 4 + SCALES * (h + 1), 0:P:HEAD_DIM],
+                    in_=scale_gain[:, HEADS_PER_HALF * h : HEADS_PER_HALF * (h + 1)],
+                )
+        table_warm = const.tile([P, 1], F32, name="table_warm")
+        nc.vector.memset(table_warm[:], 1.0)
+        nc.scalar.activation(out=table_warm[:], in_=table_warm[:], func=ACT.Exp)
+
+        x_rows = [
+            const.tile([P, TOKEN_BLOCKS, WIDTH], BF16, name="x_rows_%d" % b) for b in range(BATCH)
+        ]
+        w_rows = const.tile([P, 4, WIDTH], BF16, name="w_rows")
+        x0_blocks = x[0].rearrange("(a p) d -> p a d", p=P)
+        nc.sync.dma_start(out=x_rows[0][:, 0:2, :], in_=x0_blocks[:, 0:2, :])
+        nc.sync.dma_start(out=x_rows[0][:, 2:4, :], in_=x0_blocks[:, 2:4, :])
+        nc.sync.dma_start(out=w_rows[:, 0:2, :], in_=k_w.rearrange("(a p) d -> p a d", p=P))
+        nc.sync.dma_start(out=w_rows[:, 2:4, :], in_=v_w.rearrange("(a p) d -> p a d", p=P))
+        nc.sync.dma_start(out=x_rows[1][:], in_=x[1].rearrange("(a p) d -> p a d", p=P))
+
+        ident_f32 = const.tile([P, P], F32, name="ident_f32")
+        make_identity(nc, ident_f32[:])
+        ident_bf16 = const.tile([P, P], BF16, name="ident_bf16")
+        nc.vector.tensor_copy(out=ident_bf16[:], in_=ident_f32[:])
+        head_of = const.tile([P, HEADS_PER_HALF], F32, name="head_of")
+        nc.vector.tensor_reduce(
+            out=head_of[:],
+            in_=ident_f32[:].rearrange("p (i c) -> p i c", c=HEAD_DIM),
+            axis=AXIS.X,
+            op=ALU.add,
+        )
+        same_head = const.tile([P, HEADS_PER_HALF, HEAD_DIM], F32, name="same_head")
+        nc.vector.tensor_copy(
+            out=same_head[:],
+            in_=head_of[:].unsqueeze(2).to_broadcast([P, HEADS_PER_HALF, HEAD_DIM]),
+        )
+
+        vec_cols_ps = pools["work"].tile([P, P], BF16, name="vec_cols_ps", tag="work")
+        nc.tensor.transpose(vec_cols_ps[:], vec_rows[:], ident_bf16[:])
+        n_vec = 4 + SCALES * HALVES
+        vec_cols = const.tile([P, n_vec], F32, name="vec_cols")
+        nc.vector.tensor_copy(out=vec_cols[:], in_=vec_cols_ps[:, 0:n_vec])
+        k_bias = [vec_cols[:, h : h + 1] for h in range(HALVES)]
+        v_bias = [vec_cols[:, 2 + h : 3 + h] for h in range(HALVES)]
+        logit_ps = pools["work"].tile([P, HALVES, SCALES], F32, name="logit_ps", tag="work")
+        nc.tensor.matmul(
+            out=logit_ps[:].rearrange("p h j -> p (h j)"),
+            lhsT=same_head[:].rearrange("p i c -> p (i c)"),
+            rhs=vec_cols[:, 4:n_vec],
+            start=True,
+            stop=True,
+        )
+        shape_hj = [P, HALVES, SCALES]
+        top = const.tile([P, HALVES], F32, name="top")
+        nc.vector.tensor_reduce(out=top[:], in_=logit_ps[:], axis=AXIS.X, op=ALU.max)
+        gain = const.tile(shape_hj, F32, name="gain")
+        nc.vector.tensor_tensor(
+            out=gain[:], in0=logit_ps[:], in1=top[:].unsqueeze(2).to_broadcast(shape_hj), op=ALU.subtract
+        )
+        nc.scalar.activation(out=gain[:], in_=gain[:], func=ACT.Exp)
+        nc.scalar.activation(out=table_warm[:], in_=gain[:, 0, 0:1], func=ACT.Sqrt)
+        total = const.tile([P, HALVES], F32, name="total")
+        nc.vector.tensor_reduce(out=total[:], in_=gain[:], axis=AXIS.X, op=ALU.add)
+        nc.vector.reciprocal(out=total[:], in_=total[:])
+        nc.vector.tensor_tensor(
+            out=gain[:], in0=gain[:], in1=total[:].unsqueeze(2).to_broadcast(shape_hj), op=ALU.mult
+        )
+        n_pow2, n_triple = len(POW2_SHIFTS), len(TRIPLE_SHIFTS)
+        coef = const.tile([P, HALVES, n_pow2 + n_triple], F32, name="coef")
+        nc.vector.tensor_scalar_mul(out=coef[:, :, 0:n_pow2], in0=gain[:, :, 0:n_pow2], scalar1=TAPS[2])
+        nc.vector.scalar_tensor_tensor(
+            out=coef[:, :, 1:n_pow2],
+            in0=gain[:, :, 0 : n_pow2 - 1],
+            scalar=TAPS[1],
+            in1=coef[:, :, 1:n_pow2],
+            op0=ALU.mult,
+            op1=ALU.add,
+        )
+        nc.vector.tensor_scalar_mul(
+            out=coef[:, :, n_pow2 : n_pow2 + n_triple], in0=gain[:, :, 0:n_triple], scalar1=TAPS[0]
+        )
+        coef_over_tap3 = const.tile([P, HALVES, n_pow2 + n_triple], F32, name="coef_over_tap3")
+        nc.vector.tensor_scalar_mul(out=coef_over_tap3[:], in0=coef[:], scalar1=1.0 / TAPS[3])
+
+        x_grouped = [
+            const.tile([P, TOKENS, 4], BF16, name="x_grouped_%d" % b, align_bytes=64) for b in range(BATCH)
+        ]
+        x_codes = [const.tile([P, TOKENS], U32, name="x_codes_%d" % b, align_bytes=64) for b in range(BATCH)]
+        x_scales = [const.tile([P, TOKENS], U8, name="x_scales_%d" % b, align_bytes=64) for b in range(BATCH)]
+        w_grouped = const.tile([P, 2 * CHANNELS, 4], BF16, name="w_grouped", align_bytes=64)
+        w_codes = const.tile([P, 2 * CHANNELS], U32, name="w_codes", align_bytes=64)
+        w_scales = const.tile([P, 2 * CHANNELS], U8, name="w_scales", align_bytes=64)
+
+        def prepare_x(b):
+            for pair in range(2):
+                turn_pair(nc, pools, x_rows[b][:], pair, ident_f32[:], x_grouped[b][:])
+            quantise(nc, x_grouped[b][:], x_codes[b][:], x_scales[b][:])
+
+        def prepare_w(which):
+            cols = slice(which * CHANNELS, (which + 1) * CHANNELS)
+            turn_pair(nc, pools, w_rows[:], which, ident_f32[:], w_grouped[:])
+            quantise(nc, w_grouped[:, cols, :], w_codes[:, cols], w_scales[:, cols])
+
+        def project(b, which, h):
+            cols = slice(which * CHANNELS + h * P, which * CHANNELS + (h + 1) * P)
+            proj = pools["work"].tile([P, TOKENS], F32, name="proj", tag="work")
+            nc.tensor.matmul_mx(
+                out=proj[:],
+                lhsT=w_codes[:, cols].bitcast(FP8X4),
+                lhsT_scale=w_scales[:, cols],
+                rhs=x_codes[b][:].bitcast(FP8X4),
+                rhs_scale=x_scales[b][:],
+                start=True,
+                stop=True,
+            )
+            return proj
+
+        def make_field(b, h):
+            unit = pools["unit"]
+            k_square = unit.tile([P, TOKENS], F32, name="k_square")
+            nc.scalar.activation(
+                out=k_square[:], in_=project(b, 0, h)[:], func=ACT.Square, bias=k_bias[h], scale=1.0
+            )
+            v_full = unit.tile([P, TOKENS], F32, name="v_full")
+            nc.scalar.activation(
+                out=v_full[:], in_=project(b, 1, h)[:], func=ACT.Identity, bias=v_bias[h], scale=1.0
+            )
+            norm_ps = pools["work"].tile([P, TOKEN_BLOCKS, HEADS_PER_HALF], F32, name="norm_ps", tag="work")
+            for a in range(TOKEN_BLOCKS):
+                nc.tensor.matmul(
+                    out=norm_ps[:, a, :],
+                    lhsT=k_square[:, a * P : (a + 1) * P],
+                    rhs=head_of[:],
+                    start=True,
+                    stop=True,
+                )
+            norm = unit.tile([P, TOKEN_BLOCKS * HEADS_PER_HALF], F32, name="norm")
+            nc.scalar.activation(out=norm[:], in_=norm_ps[:].rearrange("p a i -> p (a i)"), func=ACT.Sqrt)
+            v_tok = pools["work"].tile([P, TOKEN_BLOCKS, P], F32, name="v_tok", tag="work")
+            for a in range(TOKEN_BLOCKS):
+                nc.tensor.transpose(v_tok[:, a, :], v_full[:, a * P : (a + 1) * P], ident_f32[:])
+            f_tok = unit.tile([P, TOKEN_BLOCKS, P], F32, name="f_tok")
+            nc.vector.tensor_tensor(
+                out=f_tok[:].rearrange("p a (i c) -> p (a i) c", c=HEAD_DIM),
+                in0=v_tok[:].rearrange("p a (i c) -> p (a i) c", c=HEAD_DIM),
+                in1=norm[:].unsqueeze(2).to_broadcast([P, TOKEN_BLOCKS * HEADS_PER_HALF, HEAD_DIM]),
+                op=ALU.mult,
+            )
+            field = pools["field"].tile([P, TOKENS], F32, name="field_%d_%d" % (b, h))
+            for a in range(TOKEN_BLOCKS):
+                nc.tensor.transpose(field[:, a * P : (a + 1) * P], f_tok[:, a, :], ident_f32[:])
+            base = unit.tile([P, TOKENS], F32, name="base")
+            nc.scalar.activation(out=base[:], in_=field[:], func=ACT.Copy, scale=TAPS[3])
+            return field, base
+
+        def filter_and_store(b, h, field, base):
+            unit = pools["unit"]
+            result = unit.tile([P, TOKENS], F32, name="result")
+            addend = base
+            nc.vector.tensor_copy(out=result[:, 0 : VECTOR_TERMS[0][0]], in_=base[:, 0 : VECTOR_TERMS[0][0]])
+            for shift, col in VECTOR_TERMS:
+                nc.vector.scalar_tensor_tensor(
+                    out=result[:, shift:],
+                    in0=field[:, 0 : TOKENS - shift],
+                    scalar=coef[:, h, col : col + 1],
+                    in1=addend[:, shift:],
+                    op0=ALU.mult,
+                    op1=ALU.add,
+                )
+                addend = result
+            first_shift = POOL_TERMS[0][0]
+            pool_sum = unit.tile([P, TOKENS], F32, name="pool_sum")
+            for shift, col in POOL_TERMS:
+                if shift == first_shift:
+                    scaled = pool_sum
+                else:
+                    scaled = pools["plane"].tile([P, TOKENS], F32, name="plane")
+                nc.scalar.activation(
+                    out=scaled[:, shift:],
+                    in_=base[:, 0 : TOKENS - shift],
+                    func=ACT.Copy,
+                    scale=coef_over_tap3[:, h, col : col + 1],
+                )
+                if shift != first_shift:
+                    nc.gpsimd.tensor_tensor(
+                        out=pool_sum[:, shift:], in0=pool_sum[:, shift:], in1=scaled[:, shift:], op=ALU.add
+                    )
+            nc.vector.tensor_tensor(
+                out=result[:, first_shift:], in0=result[:, first_shift:], in1=pool_sum[:, first_shift:], op=ALU.add
+            )
+            nc.sync.dma_start(out=out[b, h * P : (h + 1) * P, :], in_=result[:])
+
+        prepare_x(0)
+        prepare_w(0)
+        prepare_w(1)
+        units = [(b, h) for b in range(BATCH) for h in range(HALVES)]
+        fields = {}
+        for b, h in units:
+            if (b, h) == (1, 0):
+                prepare_x(1)
+            fields[(b, h)] = make_field(b, h)
+        for b, h in units:
+            filter_and_store(b, h, fields[(b, h)][0], fields[(b, h)][1])

@@ -33,9 +33,12 @@ VECTOR_TERMS = [term for term in TERMS if term[0] < POOL_MIN_SHIFT]
 POOL_TERMS = [term for term in TERMS if term[0] >= POOL_MIN_SHIFT]
 
 
-def turn_pair(nc, pools, rows_bf16, pair, ident_f32, grouped):
+ROUNDS = max(len(VECTOR_TERMS), len(POOL_TERMS))
+JOIN_ROUND = 2
+
+
+def turn_pair(nc, turned, rows_bf16, pair, ident_f32, grouped):
     words = rows_bf16.bitcast(F32)
-    turned = pools["work"].tile([P, 2, 2 * P], F32, name="turned", tag="work")
     for u in range(2):
         for a in range(2):
             nc.tensor.transpose(
@@ -45,7 +48,7 @@ def turn_pair(nc, pools, rows_bf16, pair, ident_f32, grouped):
             )
     nc.vector.tensor_copy(
         out=grouped.bitcast(F32)[:, 2 * pair * P : 2 * (pair + 1) * P, :],
-        in_=turned[:].rearrange("p u c -> p c u"),
+        in_=turned.rearrange("p u c -> p c u"),
     )
 
 
@@ -60,14 +63,15 @@ def tile_causalwaveletfieldattentionbyte_pa_s_kernel(
 ):
     nc = tc.nc
     with ExitStack() as stack:
-        pools = {
-            "const": stack.enter_context(tc.tile_pool(name="const", bufs=1)),
-            "unit": stack.enter_context(tc.tile_pool(name="unit", bufs=BATCH * HALVES)),
-            "plane": stack.enter_context(tc.tile_pool(name="plane", bufs=4)),
-            "work": stack.enter_context(tc.psum_pool(name="work", bufs=4)),
-            "field": stack.enter_context(tc.psum_pool(name="field", bufs=1)),
-        }
-        const = pools["const"]
+        const = stack.enter_context(tc.tile_pool(name="const", bufs=1))
+        per_batch = stack.enter_context(tc.tile_pool(name="per_batch", bufs=BATCH))
+        planes = stack.enter_context(tc.tile_pool(name="planes", bufs=3))
+        work = stack.enter_context(tc.psum_pool(name="work", bufs=4))
+        field_banks = stack.enter_context(tc.psum_pool(name="field_banks", bufs=1))
+        stack.enter_context(tc.manual_schedule())
+
+        def work_bank(shape, dtype, name):
+            return work.tile(shape, dtype, name=name, tag="work")
 
         vec_rows = const.tile([P, P], BF16, name="vec_rows")
         nc.vector.memset(vec_rows[:], 0.0)
@@ -111,14 +115,33 @@ def tile_causalwaveletfieldattentionbyte_pa_s_kernel(
             in_=head_of[:].unsqueeze(2).to_broadcast([P, HEADS_PER_HALF, HEAD_DIM]),
         )
 
-        vec_cols_ps = pools["work"].tile([P, P], BF16, name="vec_cols_ps", tag="work")
-        nc.tensor.transpose(vec_cols_ps[:], vec_rows[:], ident_bf16[:])
+        x_grouped = [
+            const.tile([P, TOKENS, 4], BF16, name="x_grouped_%d" % b, align_bytes=64) for b in range(BATCH)
+        ]
+        x_codes = [const.tile([P, TOKENS], U32, name="x_codes_%d" % b, align_bytes=64) for b in range(BATCH)]
+        x_scales = [const.tile([P, TOKENS], U8, name="x_scales_%d" % b, align_bytes=64) for b in range(BATCH)]
+        w_grouped = const.tile([P, 2 * CHANNELS, 4], BF16, name="w_grouped", align_bytes=64)
+        w_codes = const.tile([P, 2 * CHANNELS], U32, name="w_codes", align_bytes=64)
+        w_scales = const.tile([P, 2 * CHANNELS], U8, name="w_scales", align_bytes=64)
+        k_cols, v_cols = slice(0, CHANNELS), slice(CHANNELS, 2 * CHANNELS)
+        turned_shape = [P, 2, 2 * P]
+
         n_vec = 4 + SCALES * HALVES
         vec_cols = const.tile([P, n_vec], F32, name="vec_cols")
-        nc.vector.tensor_copy(out=vec_cols[:], in_=vec_cols_ps[:, 0:n_vec])
         k_bias = [vec_cols[:, h : h + 1] for h in range(HALVES)]
         v_bias = [vec_cols[:, 2 + h : 3 + h] for h in range(HALVES)]
-        logit_ps = pools["work"].tile([P, HALVES, SCALES], F32, name="logit_ps", tag="work")
+        shape_hj = [P, HALVES, SCALES]
+        gain = const.tile(shape_hj, F32, name="gain")
+
+        turn_pair(nc, work_bank(turned_shape, F32, "turned")[:], x_rows[0][:], 0, ident_f32[:], x_grouped[0][:])
+
+        vec_cols_ps = work_bank([P, P], BF16, "vec_cols_ps")
+        nc.tensor.transpose(vec_cols_ps[:], vec_rows[:], ident_bf16[:])
+        nc.vector.tensor_copy(out=vec_cols[:], in_=vec_cols_ps[:, 0:n_vec])
+
+        turn_pair(nc, work_bank(turned_shape, F32, "turned")[:], x_rows[0][:], 1, ident_f32[:], x_grouped[0][:])
+
+        logit_ps = work_bank(shape_hj, F32, "logit_ps")
         nc.tensor.matmul(
             out=logit_ps[:].rearrange("p h j -> p (h j)"),
             lhsT=same_head[:].rearrange("p i c -> p (i c)"),
@@ -126,15 +149,20 @@ def tile_causalwaveletfieldattentionbyte_pa_s_kernel(
             start=True,
             stop=True,
         )
-        shape_hj = [P, HALVES, SCALES]
         top = const.tile([P, HALVES], F32, name="top")
         nc.vector.tensor_reduce(out=top[:], in_=logit_ps[:], axis=AXIS.X, op=ALU.max)
-        gain = const.tile(shape_hj, F32, name="gain")
         nc.vector.tensor_tensor(
             out=gain[:], in0=logit_ps[:], in1=top[:].unsqueeze(2).to_broadcast(shape_hj), op=ALU.subtract
         )
         nc.scalar.activation(out=gain[:], in_=gain[:], func=ACT.Exp)
         nc.scalar.activation(out=table_warm[:], in_=gain[:, 0, 0:1], func=ACT.Sqrt)
+
+        turn_pair(nc, work_bank(turned_shape, F32, "turned")[:], w_rows[:], 0, ident_f32[:], w_grouped[:])
+        quantise(nc, x_grouped[0][:], x_codes[0][:], x_scales[0][:])
+        quantise(nc, w_grouped[:, k_cols, :], w_codes[:, k_cols], w_scales[:, k_cols])
+        turn_pair(nc, work_bank(turned_shape, F32, "turned")[:], w_rows[:], 1, ident_f32[:], w_grouped[:])
+        quantise(nc, w_grouped[:, v_cols, :], w_codes[:, v_cols], w_scales[:, v_cols])
+
         total = const.tile([P, HALVES], F32, name="total")
         nc.vector.tensor_reduce(out=total[:], in_=gain[:], axis=AXIS.X, op=ALU.add)
         nc.vector.reciprocal(out=total[:], in_=total[:])
@@ -158,122 +186,132 @@ def tile_causalwaveletfieldattentionbyte_pa_s_kernel(
         coef_over_tap3 = const.tile([P, HALVES, n_pow2 + n_triple], F32, name="coef_over_tap3")
         nc.vector.tensor_scalar_mul(out=coef_over_tap3[:], in0=coef[:], scalar1=1.0 / TAPS[3])
 
-        x_grouped = [
-            const.tile([P, TOKENS, 4], BF16, name="x_grouped_%d" % b, align_bytes=64) for b in range(BATCH)
-        ]
-        x_codes = [const.tile([P, TOKENS], U32, name="x_codes_%d" % b, align_bytes=64) for b in range(BATCH)]
-        x_scales = [const.tile([P, TOKENS], U8, name="x_scales_%d" % b, align_bytes=64) for b in range(BATCH)]
-        w_grouped = const.tile([P, 2 * CHANNELS, 4], BF16, name="w_grouped", align_bytes=64)
-        w_codes = const.tile([P, 2 * CHANNELS], U32, name="w_codes", align_bytes=64)
-        w_scales = const.tile([P, 2 * CHANNELS], U8, name="w_scales", align_bytes=64)
+        for pair in range(2):
+            turned = field_banks.tile(turned_shape, F32, name="turned_late", tag="field_1_%d" % pair)
+            turn_pair(nc, turned[:], x_rows[1][:], pair, ident_f32[:], x_grouped[1][:])
+        quantise(nc, x_grouped[1][:], x_codes[1][:], x_scales[1][:])
 
-        def prepare_x(b):
-            for pair in range(2):
-                turn_pair(nc, pools, x_rows[b][:], pair, ident_f32[:], x_grouped[b][:])
-            quantise(nc, x_grouped[b][:], x_codes[b][:], x_scales[b][:])
+        tiles = {}
+        for b in range(BATCH):
+            for name in ("k_square", "v_full", "base", "result", "pool_sum"):
+                tiles[(name, b)] = per_batch.tile([P, HALVES, TOKENS], F32, name=name)
+            tiles[("norm", b)] = per_batch.tile([P, HALVES, TOKEN_BLOCKS * HEADS_PER_HALF], F32, name="norm")
+            tiles[("f_tok", b)] = per_batch.tile([P, HALVES, TOKEN_BLOCKS, P], F32, name="f_tok")
+        fields = {}
 
-        def prepare_w(which):
-            cols = slice(which * CHANNELS, (which + 1) * CHANNELS)
-            turn_pair(nc, pools, w_rows[:], which, ident_f32[:], w_grouped[:])
-            quantise(nc, w_grouped[:, cols, :], w_codes[:, cols], w_scales[:, cols])
+        def project(b, h):
+            for first_col, func, bias, dest in (
+                (0, ACT.Square, k_bias, "k_square"),
+                (CHANNELS, ACT.Identity, v_bias, "v_full"),
+            ):
+                cols = slice(first_col + h * P, first_col + (h + 1) * P)
+                proj = work_bank([P, TOKENS], F32, "proj")
+                nc.tensor.matmul_mx(
+                    out=proj[:],
+                    lhsT=w_codes[:, cols].bitcast(FP8X4),
+                    lhsT_scale=w_scales[:, cols],
+                    rhs=x_codes[b][:].bitcast(FP8X4),
+                    rhs_scale=x_scales[b][:],
+                    start=True,
+                    stop=True,
+                )
+                nc.scalar.activation(
+                    out=tiles[(dest, b)][:, h, :], in_=proj[:], func=func, bias=bias[h], scale=1.0
+                )
 
-        def project(b, which, h):
-            cols = slice(which * CHANNELS + h * P, which * CHANNELS + (h + 1) * P)
-            proj = pools["work"].tile([P, TOKENS], F32, name="proj", tag="work")
-            nc.tensor.matmul_mx(
-                out=proj[:],
-                lhsT=w_codes[:, cols].bitcast(FP8X4),
-                lhsT_scale=w_scales[:, cols],
-                rhs=x_codes[b][:].bitcast(FP8X4),
-                rhs_scale=x_scales[b][:],
-                start=True,
-                stop=True,
-            )
-            return proj
+        v_toks = {}
 
-        def make_field(b, h):
-            unit = pools["unit"]
-            k_square = unit.tile([P, TOKENS], F32, name="k_square")
-            nc.scalar.activation(
-                out=k_square[:], in_=project(b, 0, h)[:], func=ACT.Square, bias=k_bias[h], scale=1.0
-            )
-            v_full = unit.tile([P, TOKENS], F32, name="v_full")
-            nc.scalar.activation(
-                out=v_full[:], in_=project(b, 1, h)[:], func=ACT.Identity, bias=v_bias[h], scale=1.0
-            )
-            norm_ps = pools["work"].tile([P, TOKEN_BLOCKS, HEADS_PER_HALF], F32, name="norm_ps", tag="work")
+        def norm_and_turn(b, h):
+            norm_ps = work_bank([P, TOKEN_BLOCKS, HEADS_PER_HALF], F32, "norm_ps")
             for a in range(TOKEN_BLOCKS):
                 nc.tensor.matmul(
                     out=norm_ps[:, a, :],
-                    lhsT=k_square[:, a * P : (a + 1) * P],
+                    lhsT=tiles[("k_square", b)][:, h, a * P : (a + 1) * P],
                     rhs=head_of[:],
                     start=True,
                     stop=True,
                 )
-            norm = unit.tile([P, TOKEN_BLOCKS * HEADS_PER_HALF], F32, name="norm")
-            nc.scalar.activation(out=norm[:], in_=norm_ps[:].rearrange("p a i -> p (a i)"), func=ACT.Sqrt)
-            v_tok = pools["work"].tile([P, TOKEN_BLOCKS, P], F32, name="v_tok", tag="work")
+            v_tok = work_bank([P, TOKEN_BLOCKS, P], F32, "v_tok")
             for a in range(TOKEN_BLOCKS):
-                nc.tensor.transpose(v_tok[:, a, :], v_full[:, a * P : (a + 1) * P], ident_f32[:])
-            f_tok = unit.tile([P, TOKEN_BLOCKS, P], F32, name="f_tok")
+                nc.tensor.transpose(v_tok[:, a, :], tiles[("v_full", b)][:, h, a * P : (a + 1) * P], ident_f32[:])
+            v_toks[(b, h)] = v_tok
+            nc.scalar.activation(
+                out=tiles[("norm", b)][:, h, :], in_=norm_ps[:].rearrange("p a i -> p (a i)"), func=ACT.Sqrt
+            )
+
+        def make_field(b, h):
+            f_tok = tiles[("f_tok", b)]
             nc.vector.tensor_tensor(
-                out=f_tok[:].rearrange("p a (i c) -> p (a i) c", c=HEAD_DIM),
-                in0=v_tok[:].rearrange("p a (i c) -> p (a i) c", c=HEAD_DIM),
-                in1=norm[:].unsqueeze(2).to_broadcast([P, TOKEN_BLOCKS * HEADS_PER_HALF, HEAD_DIM]),
+                out=f_tok[:, h, :, :].rearrange("p a (i c) -> p (a i) c", c=HEAD_DIM),
+                in0=v_toks[(b, h)][:].rearrange("p a (i c) -> p (a i) c", c=HEAD_DIM),
+                in1=tiles[("norm", b)][:, h, :]
+                .unsqueeze(2)
+                .to_broadcast([P, TOKEN_BLOCKS * HEADS_PER_HALF, HEAD_DIM]),
                 op=ALU.mult,
             )
-            field = pools["field"].tile([P, TOKENS], F32, name="field_%d_%d" % (b, h))
+            field = field_banks.tile([P, TOKENS], F32, name="field", tag="field_%d_%d" % (b, h))
             for a in range(TOKEN_BLOCKS):
-                nc.tensor.transpose(field[:, a * P : (a + 1) * P], f_tok[:, a, :], ident_f32[:])
-            base = unit.tile([P, TOKENS], F32, name="base")
-            nc.scalar.activation(out=base[:], in_=field[:], func=ACT.Copy, scale=TAPS[3])
-            return field, base
+                nc.tensor.transpose(field[:, a * P : (a + 1) * P], f_tok[:, h, a, :], ident_f32[:])
+            fields[(b, h)] = field
+            nc.scalar.activation(out=tiles[("base", b)][:, h, :], in_=field[:], func=ACT.Copy, scale=TAPS[3])
 
-        def filter_and_store(b, h, field, base):
-            unit = pools["unit"]
-            result = unit.tile([P, TOKENS], F32, name="result")
-            addend = base
-            nc.vector.tensor_copy(out=result[:, 0 : VECTOR_TERMS[0][0]], in_=base[:, 0 : VECTOR_TERMS[0][0]])
-            for shift, col in VECTOR_TERMS:
+        STAGES = [(stage, h) for stage in (project, norm_and_turn, make_field) for h in range(HALVES)]
+
+        def vector_term(b, r):
+            shift, col = VECTOR_TERMS[r]
+            base, result = tiles[("base", b)], tiles[("result", b)]
+            addend = base if r == 0 else result
+            for h in range(HALVES):
+                if r == 0:
+                    nc.vector.tensor_copy(out=result[:, h, 0:shift], in_=base[:, h, 0:shift])
                 nc.vector.scalar_tensor_tensor(
-                    out=result[:, shift:],
-                    in0=field[:, 0 : TOKENS - shift],
+                    out=result[:, h, shift:],
+                    in0=fields[(b, h)][:, 0 : TOKENS - shift],
                     scalar=coef[:, h, col : col + 1],
-                    in1=addend[:, shift:],
+                    in1=addend[:, h, shift:],
                     op0=ALU.mult,
                     op1=ALU.add,
                 )
-                addend = result
-            first_shift = POOL_TERMS[0][0]
-            pool_sum = unit.tile([P, TOKENS], F32, name="pool_sum")
-            for shift, col in POOL_TERMS:
-                if shift == first_shift:
-                    scaled = pool_sum
-                else:
-                    scaled = pools["plane"].tile([P, TOKENS], F32, name="plane")
+
+        def pool_term(b, r):
+            shift, col = POOL_TERMS[r]
+            pool_sum = tiles[("pool_sum", b)]
+            scaled = pool_sum if r == 0 else planes.tile([P, HALVES, TOKENS], F32, name="plane")
+            for h in range(HALVES):
                 nc.scalar.activation(
-                    out=scaled[:, shift:],
-                    in_=base[:, 0 : TOKENS - shift],
+                    out=scaled[:, h, shift:],
+                    in_=tiles[("base", b)][:, h, 0 : TOKENS - shift],
                     func=ACT.Copy,
                     scale=coef_over_tap3[:, h, col : col + 1],
                 )
-                if shift != first_shift:
-                    nc.gpsimd.tensor_tensor(
-                        out=pool_sum[:, shift:], in0=pool_sum[:, shift:], in1=scaled[:, shift:], op=ALU.add
-                    )
-            nc.vector.tensor_tensor(
-                out=result[:, first_shift:], in0=result[:, first_shift:], in1=pool_sum[:, first_shift:], op=ALU.add
-            )
-            nc.sync.dma_start(out=out[b, h * P : (h + 1) * P, :], in_=result[:])
+            if r > 0:
+                nc.gpsimd.tensor_tensor(
+                    out=pool_sum[:, :, shift:], in0=pool_sum[:, :, shift:], in1=scaled[:, :, shift:], op=ALU.add
+                )
 
-        prepare_x(0)
-        prepare_w(0)
-        prepare_w(1)
-        units = [(b, h) for b in range(BATCH) for h in range(HALVES)]
-        fields = {}
-        for b, h in units:
-            if (b, h) == (1, 0):
-                prepare_x(1)
-            fields[(b, h)] = make_field(b, h)
-        for b, h in units:
-            filter_and_store(b, h, fields[(b, h)][0], fields[(b, h)][1])
+        def join_and_store(b):
+            first_shift = POOL_TERMS[0][0]
+            result, pool_sum = tiles[("result", b)], tiles[("pool_sum", b)]
+            for h in range(HALVES):
+                nc.vector.tensor_tensor(
+                    out=result[:, h, first_shift:],
+                    in0=result[:, h, first_shift:],
+                    in1=pool_sum[:, h, first_shift:],
+                    op=ALU.add,
+                )
+                nc.sync.dma_start(out=out[b, h * P : (h + 1) * P, :], in_=result[:, h, :])
+
+        for stage, h in STAGES:
+            stage(0, h)
+        for b in range(BATCH):
+            for r in range(ROUNDS):
+                if r < len(VECTOR_TERMS):
+                    vector_term(b, r)
+                if r < len(POOL_TERMS):
+                    pool_term(b, r)
+                if b + 1 < BATCH and 1 <= r <= len(STAGES):
+                    stage, h = STAGES[r - 1]
+                    stage(b + 1, h)
+                if b > 0 and r == JOIN_ROUND:
+                    join_and_store(b - 1)
+        join_and_store(BATCH - 1)

@@ -37,7 +37,7 @@ ROUNDS = max(len(VECTOR_TERMS), len(POOL_TERMS))
 JOIN_ROUND = 2
 
 
-def turn_pair(nc, turned, rows_bf16, pair, ident_f32, grouped):
+def turn(nc, turned, rows_bf16, pair, ident_f32):
     words = rows_bf16.bitcast(F32)
     for u in range(2):
         for a in range(2):
@@ -46,7 +46,10 @@ def turn_pair(nc, turned, rows_bf16, pair, ident_f32, grouped):
                 words[:, 2 * pair + a, u * P : (u + 1) * P],
                 ident_f32,
             )
-    nc.vector.tensor_copy(
+
+
+def regroup(copy, turned, pair, grouped):
+    copy(
         out=grouped.bitcast(F32)[:, 2 * pair * P : 2 * (pair + 1) * P, :],
         in_=turned.rearrange("p u c -> p c u"),
     )
@@ -70,19 +73,25 @@ def tile_causalwaveletfieldattentionbyte_pa_s_kernel(
         field_banks = stack.enter_context(tc.psum_pool(name="field_banks", bufs=1))
         stack.enter_context(tc.manual_schedule())
 
-        def work_bank(shape, dtype, name):
-            return work.tile(shape, dtype, name=name, tag="work")
+        def work_bank(shape, name):
+            return work.tile(shape, F32, name=name, tag="work")
 
-        vec_rows = const.tile([P, P], BF16, name="vec_rows")
-        nc.vector.memset(vec_rows[:], 0.0)
-        nc.scalar.dma_start(out=vec_rows[0:2, :], in_=k_b.rearrange("(a c) -> a c", c=P))
-        nc.scalar.dma_start(out=vec_rows[2:4, :], in_=v_b.rearrange("(a c) -> a c", c=P))
-        with nc.allow_non_contiguous_dma(reason="160 gains, one to each head's first channel"):
+        def field_bank(shape, dtype, name, b, h):
+            return field_banks.tile(shape, dtype, name=name, tag="field_%d_%d" % (b, h))
+
+        logits_padded = const.tile([P, HALVES, 16], BF16, name="logits_padded")
+        nc.vector.memset(logits_padded[:], 0.0)
+        logits = logits_padded[:, :, 0:SCALES]
+        with nc.allow_non_contiguous_dma(reason="160 logits, ten to each head's first channel"):
             for h in range(HALVES):
                 nc.scalar.dma_start(
-                    out=vec_rows[4 + SCALES * h : 4 + SCALES * (h + 1), 0:P:HEAD_DIM],
-                    in_=scale_gain[:, HEADS_PER_HALF * h : HEADS_PER_HALF * (h + 1)],
+                    out=logits[0:P:HEAD_DIM, h, :],
+                    in_=scale_gain[:, h * HEADS_PER_HALF : (h + 1) * HEADS_PER_HALF].rearrange("j i -> i j"),
                 )
+        bias_rows = const.tile([P, P], BF16, name="bias_rows")
+        nc.vector.memset(bias_rows[:], 0.0)
+        nc.scalar.dma_start(out=bias_rows[0:2, :], in_=k_b.rearrange("(a c) -> a c", c=P))
+        nc.scalar.dma_start(out=bias_rows[2:4, :], in_=v_b.rearrange("(a c) -> a c", c=P))
         table_warm = const.tile([P, 1], F32, name="table_warm")
         nc.vector.memset(table_warm[:], 1.0)
         nc.scalar.activation(out=table_warm[:], in_=table_warm[:], func=ACT.Exp)
@@ -114,6 +123,8 @@ def tile_causalwaveletfieldattentionbyte_pa_s_kernel(
             out=same_head[:],
             in_=head_of[:].unsqueeze(2).to_broadcast([P, HEADS_PER_HALF, HEAD_DIM]),
         )
+        is_first = const.tile([P, 1], F32, name="is_first")
+        nc.vector.tensor_reduce(out=is_first[:], in_=ident_f32[:, 0:P:HEAD_DIM], axis=AXIS.X, op=ALU.add)
 
         x_grouped = [
             const.tile([P, TOKENS, 4], BF16, name="x_grouped_%d" % b, align_bytes=64) for b in range(BATCH)
@@ -126,70 +137,39 @@ def tile_causalwaveletfieldattentionbyte_pa_s_kernel(
         k_cols, v_cols = slice(0, CHANNELS), slice(CHANNELS, 2 * CHANNELS)
         turned_shape = [P, 2, 2 * P]
 
-        n_vec = 4 + SCALES * HALVES
-        vec_cols = const.tile([P, n_vec], F32, name="vec_cols")
-        k_bias = [vec_cols[:, h : h + 1] for h in range(HALVES)]
-        v_bias = [vec_cols[:, 2 + h : 3 + h] for h in range(HALVES)]
+        for pair, copy in ((0, nc.vector.tensor_copy), (1, nc.scalar.copy)):
+            turned = work_bank(turned_shape, "turned")
+            turn(nc, turned[:], x_rows[0][:], pair, ident_f32[:])
+            regroup(copy, turned[:], pair, x_grouped[0][:])
+
         shape_hj = [P, HALVES, SCALES]
-        gain = const.tile(shape_hj, F32, name="gain")
-
-        turn_pair(nc, work_bank(turned_shape, F32, "turned")[:], x_rows[0][:], 0, ident_f32[:], x_grouped[0][:])
-
-        vec_cols_ps = work_bank([P, P], BF16, "vec_cols_ps")
-        nc.tensor.transpose(vec_cols_ps[:], vec_rows[:], ident_bf16[:])
-        nc.vector.tensor_copy(out=vec_cols[:], in_=vec_cols_ps[:, 0:n_vec])
-
-        turn_pair(nc, work_bank(turned_shape, F32, "turned")[:], x_rows[0][:], 1, ident_f32[:], x_grouped[0][:])
-
-        logit_ps = work_bank(shape_hj, F32, "logit_ps")
-        nc.tensor.matmul(
-            out=logit_ps[:].rearrange("p h j -> p (h j)"),
-            lhsT=same_head[:].rearrange("p i c -> p (i c)"),
-            rhs=vec_cols[:, 4:n_vec],
-            start=True,
-            stop=True,
-        )
         top = const.tile([P, HALVES], F32, name="top")
-        nc.vector.tensor_reduce(out=top[:], in_=logit_ps[:], axis=AXIS.X, op=ALU.max)
+        nc.vector.tensor_reduce(out=top[:], in_=logits, axis=AXIS.X, op=ALU.max)
+        gain = const.tile(shape_hj, F32, name="gain")
         nc.vector.tensor_tensor(
-            out=gain[:], in0=logit_ps[:], in1=top[:].unsqueeze(2).to_broadcast(shape_hj), op=ALU.subtract
+            out=gain[:], in0=logits, in1=top[:].unsqueeze(2).to_broadcast(shape_hj), op=ALU.subtract
         )
         nc.scalar.activation(out=gain[:], in_=gain[:], func=ACT.Exp)
         nc.scalar.activation(out=table_warm[:], in_=gain[:, 0, 0:1], func=ACT.Sqrt)
 
-        turn_pair(nc, work_bank(turned_shape, F32, "turned")[:], w_rows[:], 0, ident_f32[:], w_grouped[:])
+        turned = work_bank(turned_shape, "turned")
+        turn(nc, turned[:], w_rows[:], 0, ident_f32[:])
+        regroup(nc.vector.tensor_copy, turned[:], 0, w_grouped[:])
         quantise(nc, x_grouped[0][:], x_codes[0][:], x_scales[0][:])
         quantise(nc, w_grouped[:, k_cols, :], w_codes[:, k_cols], w_scales[:, k_cols])
-        turn_pair(nc, work_bank(turned_shape, F32, "turned")[:], w_rows[:], 1, ident_f32[:], w_grouped[:])
+        turned = work_bank(turned_shape, "turned")
+        turn(nc, turned[:], w_rows[:], 1, ident_f32[:])
+        regroup(nc.vector.tensor_copy, turned[:], 1, w_grouped[:])
+
+        bias_ps = field_bank([P, P], BF16, "bias_ps", 0, 0)
+        nc.tensor.transpose(bias_ps[:], bias_rows[:], ident_bf16[:])
+        bias = const.tile([P, 2, HALVES], F32, name="bias")
+        nc.vector.tensor_copy(out=bias[:].rearrange("p w h -> p (w h)"), in_=bias_ps[:, 0 : 2 * HALVES])
         quantise(nc, w_grouped[:, v_cols, :], w_codes[:, v_cols], w_scales[:, v_cols])
 
-        total = const.tile([P, HALVES], F32, name="total")
-        nc.vector.tensor_reduce(out=total[:], in_=gain[:], axis=AXIS.X, op=ALU.add)
-        nc.vector.reciprocal(out=total[:], in_=total[:])
-        nc.vector.tensor_tensor(
-            out=gain[:], in0=gain[:], in1=total[:].unsqueeze(2).to_broadcast(shape_hj), op=ALU.mult
-        )
-        n_pow2, n_triple = len(POW2_SHIFTS), len(TRIPLE_SHIFTS)
-        coef = const.tile([P, HALVES, n_pow2 + n_triple], F32, name="coef")
-        nc.vector.tensor_scalar_mul(out=coef[:, :, 0:n_pow2], in0=gain[:, :, 0:n_pow2], scalar1=TAPS[2])
-        nc.vector.scalar_tensor_tensor(
-            out=coef[:, :, 1:n_pow2],
-            in0=gain[:, :, 0 : n_pow2 - 1],
-            scalar=TAPS[1],
-            in1=coef[:, :, 1:n_pow2],
-            op0=ALU.mult,
-            op1=ALU.add,
-        )
-        nc.vector.tensor_scalar_mul(
-            out=coef[:, :, n_pow2 : n_pow2 + n_triple], in0=gain[:, :, 0:n_triple], scalar1=TAPS[0]
-        )
-        coef_over_tap3 = const.tile([P, HALVES, n_pow2 + n_triple], F32, name="coef_over_tap3")
-        nc.vector.tensor_scalar_mul(out=coef_over_tap3[:], in0=coef[:], scalar1=1.0 / TAPS[3])
-
+        turned_late = [field_bank(turned_shape, F32, "turned_late", 1, pair) for pair in range(2)]
         for pair in range(2):
-            turned = field_banks.tile(turned_shape, F32, name="turned_late", tag="field_1_%d" % pair)
-            turn_pair(nc, turned[:], x_rows[1][:], pair, ident_f32[:], x_grouped[1][:])
-        quantise(nc, x_grouped[1][:], x_codes[1][:], x_scales[1][:])
+            turn(nc, turned_late[pair][:], x_rows[1][:], pair, ident_f32[:])
 
         tiles = {}
         for b in range(BATCH):
@@ -197,15 +177,14 @@ def tile_causalwaveletfieldattentionbyte_pa_s_kernel(
                 tiles[(name, b)] = per_batch.tile([P, HALVES, TOKENS], F32, name=name)
             tiles[("norm", b)] = per_batch.tile([P, HALVES, TOKEN_BLOCKS * HEADS_PER_HALF], F32, name="norm")
             tiles[("f_tok", b)] = per_batch.tile([P, HALVES, TOKEN_BLOCKS, P], F32, name="f_tok")
+        v_toks = {}
         fields = {}
 
-        def project(b, h):
-            for first_col, func, bias, dest in (
-                (0, ACT.Square, k_bias, "k_square"),
-                (CHANNELS, ACT.Identity, v_bias, "v_full"),
-            ):
-                cols = slice(first_col + h * P, first_col + (h + 1) * P)
-                proj = work_bank([P, TOKENS], F32, "proj")
+        def project(b, which):
+            func, dest = ((ACT.Square, "k_square"), (ACT.Identity, "v_full"))[which]
+            for h in range(HALVES):
+                cols = slice(which * CHANNELS + h * P, which * CHANNELS + (h + 1) * P)
+                proj = work_bank([P, TOKENS], "proj")
                 nc.tensor.matmul_mx(
                     out=proj[:],
                     lhsT=w_codes[:, cols].bitcast(FP8X4),
@@ -216,13 +195,11 @@ def tile_causalwaveletfieldattentionbyte_pa_s_kernel(
                     stop=True,
                 )
                 nc.scalar.activation(
-                    out=tiles[(dest, b)][:, h, :], in_=proj[:], func=func, bias=bias[h], scale=1.0
+                    out=tiles[(dest, b)][:, h, :], in_=proj[:], func=func, bias=bias[:, which, h : h + 1], scale=1.0
                 )
 
-        v_toks = {}
-
-        def norm_and_turn(b, h):
-            norm_ps = work_bank([P, TOKEN_BLOCKS, HEADS_PER_HALF], F32, "norm_ps")
+        def norm(b, h):
+            norm_ps = work_bank([P, TOKEN_BLOCKS, HEADS_PER_HALF], "norm_ps")
             for a in range(TOKEN_BLOCKS):
                 nc.tensor.matmul(
                     out=norm_ps[:, a, :],
@@ -231,13 +208,18 @@ def tile_causalwaveletfieldattentionbyte_pa_s_kernel(
                     start=True,
                     stop=True,
                 )
-            v_tok = work_bank([P, TOKEN_BLOCKS, P], F32, "v_tok")
-            for a in range(TOKEN_BLOCKS):
-                nc.tensor.transpose(v_tok[:, a, :], tiles[("v_full", b)][:, h, a * P : (a + 1) * P], ident_f32[:])
-            v_toks[(b, h)] = v_tok
             nc.scalar.activation(
                 out=tiles[("norm", b)][:, h, :], in_=norm_ps[:].rearrange("p a i -> p (a i)"), func=ACT.Sqrt
             )
+
+        def turn_v(b):
+            for h in range(HALVES):
+                v_tok = work_bank([P, TOKEN_BLOCKS, P], "v_tok")
+                for a in range(TOKEN_BLOCKS):
+                    nc.tensor.transpose(
+                        v_tok[:, a, :], tiles[("v_full", b)][:, h, a * P : (a + 1) * P], ident_f32[:]
+                    )
+                v_toks[(b, h)] = v_tok
 
         def make_field(b, h):
             f_tok = tiles[("f_tok", b)]
@@ -249,13 +231,67 @@ def tile_causalwaveletfieldattentionbyte_pa_s_kernel(
                 .to_broadcast([P, TOKEN_BLOCKS * HEADS_PER_HALF, HEAD_DIM]),
                 op=ALU.mult,
             )
-            field = field_banks.tile([P, TOKENS], F32, name="field", tag="field_%d_%d" % (b, h))
+            field = field_bank([P, TOKENS], F32, "field", b, h)
             for a in range(TOKEN_BLOCKS):
                 nc.tensor.transpose(field[:, a * P : (a + 1) * P], f_tok[:, h, a, :], ident_f32[:])
             fields[(b, h)] = field
             nc.scalar.activation(out=tiles[("base", b)][:, h, :], in_=field[:], func=ACT.Copy, scale=TAPS[3])
 
-        STAGES = [(stage, h) for stage in (project, norm_and_turn, make_field) for h in range(HALVES)]
+        def stages(b):
+            return [
+                lambda: project(b, 0),
+                lambda: project(b, 1),
+                lambda: norm(b, 0),
+                lambda: norm(b, 1),
+                lambda: turn_v(b),
+                lambda: make_field(b, 0),
+                lambda: make_field(b, 1),
+            ]
+
+        first = stages(0)
+        first[0]()
+        first[1]()
+
+        total = const.tile([P, HALVES], F32, name="total")
+        nc.vector.tensor_reduce(out=total[:], in_=gain[:], axis=AXIS.X, op=ALU.add)
+        nc.vector.reciprocal(out=total[:], in_=total[:])
+        nc.vector.tensor_scalar_mul(out=total[:], in0=total[:], scalar1=is_first[:, 0:1])
+        nc.vector.tensor_tensor(
+            out=gain[:], in0=gain[:], in1=total[:].unsqueeze(2).to_broadcast(shape_hj), op=ALU.mult
+        )
+        n_pow2, n_triple = len(POW2_SHIFTS), len(TRIPLE_SHIFTS)
+        table_shape = [P, 2, HALVES, n_pow2 + n_triple]
+        by_head = const.tile(table_shape, F32, name="by_head")
+        nc.vector.tensor_scalar_mul(out=by_head[:, 0, :, 0:n_pow2], in0=gain[:, :, 0:n_pow2], scalar1=TAPS[2])
+        nc.vector.scalar_tensor_tensor(
+            out=by_head[:, 0, :, 1:n_pow2],
+            in0=gain[:, :, 0 : n_pow2 - 1],
+            scalar=TAPS[1],
+            in1=by_head[:, 0, :, 1:n_pow2],
+            op0=ALU.mult,
+            op1=ALU.add,
+        )
+        nc.vector.tensor_scalar_mul(out=by_head[:, 0, :, n_pow2:], in0=gain[:, :, 0:n_triple], scalar1=TAPS[0])
+        nc.vector.tensor_scalar_mul(out=by_head[:, 1, :, :], in0=by_head[:, 0, :, :], scalar1=1.0 / TAPS[3])
+        for pair in range(2):
+            regroup(nc.vector.tensor_copy, turned_late[pair][:], pair, x_grouped[1][:])
+        quantise(nc, x_grouped[1][:], x_codes[1][:], x_scales[1][:])
+
+        for stage in first[2:5]:
+            stage()
+        by_channel_ps = field_bank(table_shape, F32, "by_channel_ps", 1, 0)
+        nc.tensor.matmul(
+            out=by_channel_ps[:].rearrange("p k h t -> p (k h t)"),
+            lhsT=same_head[:].rearrange("p i c -> p (i c)"),
+            rhs=by_head[:].rearrange("p k h t -> p (k h t)"),
+            start=True,
+            stop=True,
+        )
+        for stage in first[5:]:
+            stage()
+        by_channel = const.tile(table_shape, F32, name="by_channel")
+        nc.vector.tensor_copy(out=by_channel[:], in_=by_channel_ps[:])
+        coef, coef_over_tap3 = by_channel[:, 0, :, :], by_channel[:, 1, :, :]
 
         def vector_term(b, r):
             shift, col = VECTOR_TERMS[r]
@@ -301,17 +337,15 @@ def tile_causalwaveletfieldattentionbyte_pa_s_kernel(
                 )
                 nc.sync.dma_start(out=out[b, h * P : (h + 1) * P, :], in_=result[:, h, :])
 
-        for stage, h in STAGES:
-            stage(0, h)
         for b in range(BATCH):
+            later = stages(b + 1) if b + 1 < BATCH else []
             for r in range(ROUNDS):
                 if r < len(VECTOR_TERMS):
                     vector_term(b, r)
                 if r < len(POOL_TERMS):
                     pool_term(b, r)
-                if b + 1 < BATCH and 1 <= r <= len(STAGES):
-                    stage, h = STAGES[r - 1]
-                    stage(b + 1, h)
+                if 1 <= r <= len(later):
+                    later[r - 1]()
                 if b > 0 and r == JOIN_ROUND:
                     join_and_store(b - 1)
         join_and_store(BATCH - 1)

@@ -125,6 +125,10 @@ def tile_causalwaveletfieldattentionbyte_pa_s_kernel(
         )
         is_first = const.tile([P, 1], F32, name="is_first")
         nc.vector.tensor_reduce(out=is_first[:], in_=ident_f32[:, 0:P:HEAD_DIM], axis=AXIS.X, op=ALU.add)
+        spread = const.tile([P, P], F32, name="spread")
+        nc.vector.tensor_scalar_mul(
+            out=spread[:], in0=same_head[:].rearrange("p i c -> p (i c)"), scalar1=is_first[:, 0:1]
+        )
 
         x_grouped = [
             const.tile([P, TOKENS, 4], BF16, name="x_grouped_%d" % b, align_bytes=64) for b in range(BATCH)
@@ -143,13 +147,19 @@ def tile_causalwaveletfieldattentionbyte_pa_s_kernel(
             regroup(copy, turned[:], pair, x_grouped[0][:])
 
         shape_hj = [P, HALVES, SCALES]
-        top = const.tile([P, HALVES], F32, name="top")
-        nc.vector.tensor_reduce(out=top[:], in_=logits, axis=AXIS.X, op=ALU.max)
+        minus_top = const.tile([P, HALVES], F32, name="minus_top")
+        nc.vector.tensor_reduce(out=minus_top[:], in_=logits, axis=AXIS.X, op=ALU.max, negate=True)
         gain = const.tile(shape_hj, F32, name="gain")
-        nc.vector.tensor_tensor(
-            out=gain[:], in0=logits, in1=top[:].unsqueeze(2).to_broadcast(shape_hj), op=ALU.subtract
-        )
-        nc.scalar.activation(out=gain[:], in_=gain[:], func=ACT.Exp)
+        total = const.tile([P, HALVES, 8], F32, name="total")
+        for h in range(HALVES):
+            nc.scalar.activation(
+                out=gain[:, h, :],
+                in_=logits[:, h, :],
+                func=ACT.Exp,
+                bias=minus_top[:, h : h + 1],
+                scale=1.0,
+                accum_out=total[:, h, 0:1],
+            )
         nc.scalar.activation(out=table_warm[:], in_=gain[:, 0, 0:1], func=ACT.Sqrt)
 
         turned = work_bank(turned_shape, "turned")
@@ -252,46 +262,43 @@ def tile_causalwaveletfieldattentionbyte_pa_s_kernel(
         first[0]()
         first[1]()
 
-        total = const.tile([P, HALVES], F32, name="total")
-        nc.vector.tensor_reduce(out=total[:], in_=gain[:], axis=AXIS.X, op=ALU.add)
-        nc.vector.reciprocal(out=total[:], in_=total[:])
-        nc.vector.tensor_scalar_mul(out=total[:], in0=total[:], scalar1=is_first[:, 0:1])
-        nc.vector.tensor_tensor(
-            out=gain[:], in0=gain[:], in1=total[:].unsqueeze(2).to_broadcast(shape_hj), op=ALU.mult
-        )
         n_pow2, n_triple = len(POW2_SHIFTS), len(TRIPLE_SHIFTS)
-        table_shape = [P, 2, HALVES, n_pow2 + n_triple]
+        table_shape = [P, HALVES, n_pow2 + n_triple]
         by_head = const.tile(table_shape, F32, name="by_head")
-        nc.vector.tensor_scalar_mul(out=by_head[:, 0, :, 0:n_pow2], in0=gain[:, :, 0:n_pow2], scalar1=TAPS[2])
+        nc.vector.reciprocal(out=total[:, :, 0:1], in_=total[:, :, 0:1])
+        regroup(nc.vector.tensor_copy, turned_late[0][:], 0, x_grouped[1][:])
+        nc.vector.tensor_tensor(
+            out=gain[:], in0=gain[:], in1=total[:, :, 0:1].to_broadcast(shape_hj), op=ALU.mult
+        )
+        regroup(nc.vector.tensor_copy, turned_late[1][:], 1, x_grouped[1][:])
+        nc.vector.tensor_scalar_mul(out=by_head[:, :, 0:n_pow2], in0=gain[:, :, 0:n_pow2], scalar1=TAPS[2])
+        nc.vector.tensor_scalar_mul(out=by_head[:, :, n_pow2:], in0=gain[:, :, 0:n_triple], scalar1=TAPS[0])
+        quantise(nc, x_grouped[1][:], x_codes[1][:], x_scales[1][:])
         nc.vector.scalar_tensor_tensor(
-            out=by_head[:, 0, :, 1:n_pow2],
+            out=by_head[:, :, 1:n_pow2],
             in0=gain[:, :, 0 : n_pow2 - 1],
             scalar=TAPS[1],
-            in1=by_head[:, 0, :, 1:n_pow2],
+            in1=by_head[:, :, 1:n_pow2],
             op0=ALU.mult,
             op1=ALU.add,
         )
-        nc.vector.tensor_scalar_mul(out=by_head[:, 0, :, n_pow2:], in0=gain[:, :, 0:n_triple], scalar1=TAPS[0])
-        nc.vector.tensor_scalar_mul(out=by_head[:, 1, :, :], in0=by_head[:, 0, :, :], scalar1=1.0 / TAPS[3])
-        for pair in range(2):
-            regroup(nc.vector.tensor_copy, turned_late[pair][:], pair, x_grouped[1][:])
-        quantise(nc, x_grouped[1][:], x_codes[1][:], x_scales[1][:])
 
         for stage in first[2:5]:
             stage()
         by_channel_ps = field_bank(table_shape, F32, "by_channel_ps", 1, 0)
         nc.tensor.matmul(
-            out=by_channel_ps[:].rearrange("p k h t -> p (k h t)"),
-            lhsT=same_head[:].rearrange("p i c -> p (i c)"),
-            rhs=by_head[:].rearrange("p k h t -> p (k h t)"),
+            out=by_channel_ps[:].rearrange("p h t -> p (h t)"),
+            lhsT=spread[:],
+            rhs=by_head[:].rearrange("p h t -> p (h t)"),
             start=True,
             stop=True,
         )
         for stage in first[5:]:
             stage()
-        by_channel = const.tile(table_shape, F32, name="by_channel")
-        nc.vector.tensor_copy(out=by_channel[:], in_=by_channel_ps[:])
-        coef, coef_over_tap3 = by_channel[:, 0, :, :], by_channel[:, 1, :, :]
+        coef = const.tile(table_shape, F32, name="coef")
+        nc.vector.tensor_copy(out=coef[:], in_=by_channel_ps[:])
+        coef_over_tap3 = const.tile(table_shape, F32, name="coef_over_tap3")
+        nc.vector.tensor_scalar_mul(out=coef_over_tap3[:], in0=by_channel_ps[:], scalar1=1.0 / TAPS[3])
 
         def vector_term(b, r):
             shift, col = VECTOR_TERMS[r]

from contextlib import ExitStack

import concourse.mybir as mybir
from concourse.masks import make_identity

F32 = mybir.dt.float32
BF16 = mybir.dt.bfloat16
U32 = mybir.dt.uint32
U8 = mybir.dt.uint8
FP8X4 = mybir.dt.float8_e4m3fn_x4
ALU = mybir.AluOpType
ACT = mybir.ActivationFunctionType
AXIS = mybir.AxisListType

P = 128
BATCH, TOKENS, WIDTH, CHANNELS, HEADS, SCALES = 2, 512, 512, 256, 16, 10
HEAD_DIM = CHANNELS // HEADS
HALVES = CHANNELS // P
HEADS_PER_HALF = P // HEAD_DIM
TOKEN_BLOCKS = TOKENS // P
TAPS = (0.4829629131445341, 0.8365163037378079, 0.2241438680420134, -0.1294095225512604)

FLOPS = 2 * BATCH * TOKENS * WIDTH * 2 * CHANNELS

POW2_SHIFTS = [2**i for i in range(SCALES) if 2**i < TOKENS]
TRIPLE_SHIFTS = [3 * 2**j for j in range(SCALES) if 3 * 2**j < TOKENS]
TERMS = sorted(
    [(s, i) for i, s in enumerate(POW2_SHIFTS)]
    + [(s, len(POW2_SHIFTS) + j) for j, s in enumerate(TRIPLE_SHIFTS)]
)
POOL_MIN_SHIFT = 48
VECTOR_TERMS = [term for term in TERMS if term[0] < POOL_MIN_SHIFT]
POOL_TERMS = [term for term in TERMS if term[0] >= POOL_MIN_SHIFT]


ROUNDS = max(len(VECTOR_TERMS), len(POOL_TERMS))
JOIN_ROUND = 2


def turn(nc, turned, rows_bf16, pair, ident_f32):
    words = rows_bf16.bitcast(F32)
    for u in range(2):
        for a in range(2):
            nc.tensor.transpose(
                turned[:, u, a * P : (a + 1) * P],
                words[:, 2 * pair + a, u * P : (u + 1) * P],
                ident_f32,
            )


def regroup(copy, turned, pair, grouped):
    copy(
        out=grouped.bitcast(F32)[:, 2 * pair * P : 2 * (pair + 1) * P, :],
        in_=turned.rearrange("p u c -> p c u"),
    )


def quantise(nc, grouped, codes, scales):
    nc.vector.quantize_mx(
        out=codes.bitcast(FP8X4), scales=scales, in_=grouped.rearrange("p c t -> p (c t)")
    )


def tile_causalwaveletfieldattentionbyte_pa_s_kernel(
    tc, x, k_w, k_b, v_w, v_b, scale_gain, out
):
    nc = tc.nc
    with ExitStack() as stack:
        const = stack.enter_context(tc.tile_pool(name="const", bufs=1))
        per_batch = stack.enter_context(tc.tile_pool(name="per_batch", bufs=BATCH))
        planes = stack.enter_context(tc.tile_pool(name="planes", bufs=3))
        work = stack.enter_context(tc.psum_pool(name="work", bufs=4))
        field_banks = stack.enter_context(tc.psum_pool(name="field_banks", bufs=1))
        stack.enter_context(tc.manual_schedule())

        def work_bank(shape, name):
            return work.tile(shape, F32, name=name, tag="work")

        def field_bank(shape, dtype, name, b, h):
            return field_banks.tile(shape, dtype, name=name, tag="field_%d_%d" % (b, h))

        logits_padded = const.tile([P, HALVES, 16], BF16, name="logits_padded")
        nc.vector.memset(logits_padded[:], 0.0)
        logits = logits_padded[:, :, 0:SCALES]
        with nc.allow_non_contiguous_dma(reason="160 logits, ten to each head's first channel"):
            for h in range(HALVES):
                nc.scalar.dma_start(
                    out=logits[0:P:HEAD_DIM, h, :],
                    in_=scale_gain[:, h * HEADS_PER_HALF : (h + 1) * HEADS_PER_HALF].rearrange("j i -> i j"),
                )
        bias_rows = const.tile([P, P], BF16, name="bias_rows")
        nc.vector.memset(bias_rows[:], 0.0)
        nc.scalar.dma_start(out=bias_rows[0:2, :], in_=k_b.rearrange("(a c) -> a c", c=P))
        nc.scalar.dma_start(out=bias_rows[2:4, :], in_=v_b.rearrange("(a c) -> a c", c=P))
        table_warm = const.tile([P, 1], F32, name="table_warm")
        nc.vector.memset(table_warm[:], 1.0)
        nc.scalar.activation(out=table_warm[:], in_=table_warm[:], func=ACT.Exp)

        x_rows = [
            const.tile([P, TOKEN_BLOCKS, WIDTH], BF16, name="x_rows_%d" % b) for b in range(BATCH)
        ]
        w_rows = const.tile([P, 4, WIDTH], BF16, name="w_rows")
        x0_blocks = x[0].rearrange("(a p) d -> p a d", p=P)
        nc.sync.dma_start(out=x_rows[0][:, 0:2, :], in_=x0_blocks[:, 0:2, :])
        nc.sync.dma_start(out=x_rows[0][:, 2:4, :], in_=x0_blocks[:, 2:4, :])
        nc.sync.dma_start(out=w_rows[:, 0:2, :], in_=k_w.rearrange("(a p) d -> p a d", p=P))
        nc.sync.dma_start(out=w_rows[:, 2:4, :], in_=v_w.rearrange("(a p) d -> p a d", p=P))
        nc.sync.dma_start(out=x_rows[1][:], in_=x[1].rearrange("(a p) d -> p a d", p=P))

        ident_f32 = const.tile([P, P], F32, name="ident_f32")
        make_identity(nc, ident_f32[:])
        ident_bf16 = const.tile([P, P], BF16, name="ident_bf16")
        nc.vector.tensor_copy(out=ident_bf16[:], in_=ident_f32[:])
        head_of = const.tile([P, HEADS_PER_HALF], F32, name="head_of")
        nc.vector.tensor_reduce(
            out=head_of[:],
            in_=ident_f32[:].rearrange("p (i c) -> p i c", c=HEAD_DIM),
            axis=AXIS.X,
            op=ALU.add,
        )
        same_head = const.tile([P, HEADS_PER_HALF, HEAD_DIM], F32, name="same_head")
        nc.vector.tensor_copy(
            out=same_head[:],
            in_=head_of[:].unsqueeze(2).to_broadcast([P, HEADS_PER_HALF, HEAD_DIM]),
        )
        is_first = const.tile([P, 1], F32, name="is_first")
        nc.vector.tensor_reduce(out=is_first[:], in_=ident_f32[:, 0:P:HEAD_DIM], axis=AXIS.X, op=ALU.add)
        spread = const.tile([P, P], F32, name="spread")
        nc.vector.tensor_scalar_mul(
            out=spread[:], in0=same_head[:].rearrange("p i c -> p (i c)"), scalar1=is_first[:, 0:1]
        )

        x_grouped = [
            const.tile([P, TOKENS, 4], BF16, name="x_grouped_%d" % b, align_bytes=64) for b in range(BATCH)
        ]
        x_codes = [const.tile([P, TOKENS], U32, name="x_codes_%d" % b, align_bytes=64) for b in range(BATCH)]
        x_scales = [const.tile([P, TOKENS], U8, name="x_scales_%d" % b, align_bytes=64) for b in range(BATCH)]
        w_grouped = const.tile([P, 2 * CHANNELS, 4], BF16, name="w_grouped", align_bytes=64)
        w_codes = const.tile([P, 2 * CHANNELS], U32, name="w_codes", align_bytes=64)
        w_scales = const.tile([P, 2 * CHANNELS], U8, name="w_scales", align_bytes=64)
        k_cols, v_cols = slice(0, CHANNELS), slice(CHANNELS, 2 * CHANNELS)
        turned_shape = [P, 2, 2 * P]

        for pair, copy in ((0, nc.vector.tensor_copy), (1, nc.scalar.copy)):
            turned = work_bank(turned_shape, "turned")
            turn(nc, turned[:], x_rows[0][:], pair, ident_f32[:])
            regroup(copy, turned[:], pair, x_grouped[0][:])

        shape_hj = [P, HALVES, SCALES]
        minus_top = const.tile([P, HALVES], F32, name="minus_top")
        nc.vector.tensor_reduce(out=minus_top[:], in_=logits, axis=AXIS.X, op=ALU.max, negate=True)
        gain = const.tile(shape_hj, F32, name="gain")
        total = const.tile([P, HALVES, 8], F32, name="total")
        for h in range(HALVES):
            nc.scalar.activation(
                out=gain[:, h, :],
                in_=logits[:, h, :],
                func=ACT.Exp,
                bias=minus_top[:, h : h + 1],
                scale=1.0,
                accum_out=total[:, h, 0:1],
            )
        nc.scalar.activation(out=table_warm[:], in_=gain[:, 0, 0:1], func=ACT.Sqrt)

        turned = work_bank(turned_shape, "turned")
        turn(nc, turned[:], w_rows[:], 0, ident_f32[:])
        regroup(nc.vector.tensor_copy, turned[:], 0, w_grouped[:])
        quantise(nc, x_grouped[0][:], x_codes[0][:], x_scales[0][:])
        quantise(nc, w_grouped[:, k_cols, :], w_codes[:, k_cols], w_scales[:, k_cols])
        turned = work_bank(turned_shape, "turned")
        turn(nc, turned[:], w_rows[:], 1, ident_f32[:])
        regroup(nc.vector.tensor_copy, turned[:], 1, w_grouped[:])

        bias_ps = field_bank([P, P], BF16, "bias_ps", 0, 0)
        nc.tensor.transpose(bias_ps[:], bias_rows[:], ident_bf16[:])
        bias = const.tile([P, 2, HALVES], F32, name="bias")
        nc.vector.tensor_copy(out=bias[:].rearrange("p w h -> p (w h)"), in_=bias_ps[:, 0 : 2 * HALVES])
        quantise(nc, w_grouped[:, v_cols, :], w_codes[:, v_cols], w_scales[:, v_cols])

        turned_late = [field_bank(turned_shape, F32, "turned_late", 1, pair) for pair in range(2)]
        for pair in range(2):
            turn(nc, turned_late[pair][:], x_rows[1][:], pair, ident_f32[:])

        tiles = {}
        for b in range(BATCH):
            for name in ("k_square", "v_full", "base", "result", "pool_sum"):
                tiles[(name, b)] = per_batch.tile([P, HALVES, TOKENS], F32, name=name)
            tiles[("norm", b)] = per_batch.tile([P, HALVES, TOKEN_BLOCKS * HEADS_PER_HALF], F32, name="norm")
            tiles[("f_tok", b)] = per_batch.tile([P, HALVES, TOKEN_BLOCKS, P], F32, name="f_tok")
        v_toks = {}
        fields = {}

        def project(b, which):
            func, dest = ((ACT.Square, "k_square"), (ACT.Identity, "v_full"))[which]
            for h in range(HALVES):
                cols = slice(which * CHANNELS + h * P, which * CHANNELS + (h + 1) * P)
                proj = work_bank([P, TOKENS], "proj")
                nc.tensor.matmul_mx(
                    out=proj[:],
                    lhsT=w_codes[:, cols].bitcast(FP8X4),
                    lhsT_scale=w_scales[:, cols],
                    rhs=x_codes[b][:].bitcast(FP8X4),
                    rhs_scale=x_scales[b][:],
                    start=True,
                    stop=True,
                )
                nc.scalar.activation(
                    out=tiles[(dest, b)][:, h, :], in_=proj[:], func=func, bias=bias[:, which, h : h + 1], scale=1.0
                )

        def norm(b, h):
            norm_ps = work_bank([P, TOKEN_BLOCKS, HEADS_PER_HALF], "norm_ps")
            for a in range(TOKEN_BLOCKS):
                nc.tensor.matmul(
                    out=norm_ps[:, a, :],
                    lhsT=tiles[("k_square", b)][:, h, a * P : (a + 1) * P],
                    rhs=head_of[:],
                    start=True,
                    stop=True,
                )
            nc.scalar.activation(
                out=tiles[("norm", b)][:, h, :], in_=norm_ps[:].rearrange("p a i -> p (a i)"), func=ACT.Sqrt
            )

        def turn_v(b):
            for h in range(HALVES):
                v_tok = work_bank([P, TOKEN_BLOCKS, P], "v_tok")
                for a in range(TOKEN_BLOCKS):
                    nc.tensor.transpose(
                        v_tok[:, a, :], tiles[("v_full", b)][:, h, a * P : (a + 1) * P], ident_f32[:]
                    )
                v_toks[(b, h)] = v_tok

        def make_field(b, h):
            f_tok = tiles[("f_tok", b)]
            nc.vector.tensor_tensor(
                out=f_tok[:, h, :, :].rearrange("p a (i c) -> p (a i) c", c=HEAD_DIM),
                in0=v_toks[(b, h)][:].rearrange("p a (i c) -> p (a i) c", c=HEAD_DIM),
                in1=tiles[("norm", b)][:, h, :]
                .unsqueeze(2)
                .to_broadcast([P, TOKEN_BLOCKS * HEADS_PER_HALF, HEAD_DIM]),
                op=ALU.mult,
            )
            field = field_bank([P, TOKENS], F32, "field", b, h)
            for a in range(TOKEN_BLOCKS):
                nc.tensor.transpose(field[:, a * P : (a + 1) * P], f_tok[:, h, a, :], ident_f32[:])
            fields[(b, h)] = field
            nc.scalar.activation(out=tiles[("base", b)][:, h, :], in_=field[:], func=ACT.Copy, scale=TAPS[3])

        def stages(b):
            return [
                lambda: project(b, 0),
                lambda: project(b, 1),
                lambda: norm(b, 0),
                lambda: norm(b, 1),
                lambda: turn_v(b),
                lambda: make_field(b, 0),
                lambda: make_field(b, 1),
            ]

        first = stages(0)
        first[0]()
        first[1]()

        n_pow2, n_triple = len(POW2_SHIFTS), len(TRIPLE_SHIFTS)
        table_shape = [P, HALVES, n_pow2 + n_triple]
        by_head = const.tile(table_shape, F32, name="by_head")
        nc.vector.reciprocal(out=total[:, :, 0:1], in_=total[:, :, 0:1])
        regroup(nc.vector.tensor_copy, turned_late[0][:], 0, x_grouped[1][:])
        nc.vector.tensor_tensor(
            out=gain[:], in0=gain[:], in1=total[:, :, 0:1].to_broadcast(shape_hj), op=ALU.mult
        )
        regroup(nc.vector.tensor_copy, turned_late[1][:], 1, x_grouped[1][:])
        nc.vector.tensor_scalar_mul(out=by_head[:, :, 0:n_pow2], in0=gain[:, :, 0:n_pow2], scalar1=TAPS[2])
        nc.vector.tensor_scalar_mul(out=by_head[:, :, n_pow2:], in0=gain[:, :, 0:n_triple], scalar1=TAPS[0])
        quantise(nc, x_grouped[1][:], x_codes[1][:], x_scales[1][:])
        nc.vector.scalar_tensor_tensor(
            out=by_head[:, :, 1:n_pow2],
            in0=gain[:, :, 0 : n_pow2 - 1],
            scalar=TAPS[1],
            in1=by_head[:, :, 1:n_pow2],
            op0=ALU.mult,
            op1=ALU.add,
        )

        for stage in first[2:5]:
            stage()
        by_channel_ps = field_bank(table_shape, F32, "by_channel_ps", 1, 0)
        nc.tensor.matmul(
            out=by_channel_ps[:].rearrange("p h t -> p (h t)"),
            lhsT=spread[:],
            rhs=by_head[:].rearrange("p h t -> p (h t)"),
            start=True,
            stop=True,
        )
        for stage in first[5:]:
            stage()
        coef = const.tile(table_shape, F32, name="coef")
        nc.vector.tensor_copy(out=coef[:], in_=by_channel_ps[:])
        coef_over_tap3 = const.tile(table_shape, F32, name="coef_over_tap3")
        nc.vector.tensor_scalar_mul(out=coef_over_tap3[:], in0=by_channel_ps[:], scalar1=1.0 / TAPS[3])

        def vector_term(b, r):
            shift, col = VECTOR_TERMS[r]
            base, result = tiles[("base", b)], tiles[("result", b)]
            addend = base if r == 0 else result
            for h in range(HALVES):
                if r == 0:
                    nc.vector.tensor_copy(out=result[:, h, 0:shift], in_=base[:, h, 0:shift])
                nc.vector.scalar_tensor_tensor(
                    out=result[:, h, shift:],
                    in0=fields[(b, h)][:, 0 : TOKENS - shift],
                    scalar=coef[:, h, col : col + 1],
                    in1=addend[:, h, shift:],
                    op0=ALU.mult,
                    op1=ALU.add,
                )

        def pool_term(b, r):
            shift, col = POOL_TERMS[r]
            pool_sum = tiles[("pool_sum", b)]
            scaled = pool_sum if r == 0 else planes.tile([P, HALVES, TOKENS], F32, name="plane")
            for h in range(HALVES):
                nc.scalar.activation(
                    out=scaled[:, h, shift:],
                    in_=tiles[("base", b)][:, h, 0 : TOKENS - shift],
                    func=ACT.Copy,
                    scale=coef_over_tap3[:, h, col : col + 1],
                )
            if r > 0:
                nc.gpsimd.tensor_tensor(
                    out=pool_sum[:, :, shift:], in0=pool_sum[:, :, shift:], in1=scaled[:, :, shift:], op=ALU.add
                )

        def join_and_store(b):
            first_shift = POOL_TERMS[0][0]
            result, pool_sum = tiles[("result", b)], tiles[("pool_sum", b)]
            for h in range(HALVES):
                nc.vector.tensor_tensor(
                    out=result[:, h, first_shift:],
                    in0=result[:, h, first_shift:],
                    in1=pool_sum[:, h, first_shift:],
                    op=ALU.add,
                )
                nc.sync.dma_start(out=out[b, h * P : (h + 1) * P, :], in_=result[:, h, :])

        for b in range(BATCH):
            later = stages(b + 1) if b + 1 < BATCH else []
            for r in range(ROUNDS):
                if r < len(VECTOR_TERMS):
                    vector_term(b, r)
                if r < len(POOL_TERMS):
                    pool_term(b, r)
                if 1 <= r <= len(later):
                    later[r - 1]()
                if b > 0 and r == JOIN_ROUND:
                    join_and_store(b - 1)
        join_and_store(BATCH - 1)
